import numpy as np
import ml_dtypes


def mxq(x, axis, fmt="e4m3"):
    dtype, down = {"e4m3": (ml_dtypes.float8_e4m3fn, 7), "e5m2": (ml_dtypes.float8_e5m2, 14)}[fmt]
    v = np.moveaxis(np.asarray(x, np.float32).astype(ml_dtypes.bfloat16).astype(np.float64), axis, -1)
    blocks = v.reshape(v.shape[:-1] + (-1, 32))
    amax = np.abs(blocks).max(-1, keepdims=True)
    byte = np.maximum(np.where(amax > 0, np.frexp(amax)[1] - 1 + 127, 0) - down, 1)
    scale = np.exp2(byte - 127.0)
    codes = (blocks / scale).astype(np.float32).astype(dtype).astype(np.float64)
    return np.moveaxis((codes * scale).reshape(v.shape), -1, axis)


WIDE = False


def mx_kscale(k):
    if not WIDE:
        return np.ones(k)
    levels = np.array([10, -10, 5, -5, 0])
    if k % 512:
        return np.exp2(np.random.permutation(np.resize(levels, k // 32))).repeat(32)
    a = np.empty((k // 512, 16))
    for p in range(k // 512):
        a[p, :8] = np.random.permutation(np.resize(levels, 8))
        for g in range(8):
            far = levels[np.abs(levels - a[p, g]) >= 10]
            a[p, g + 8] = far[np.random.randint(len(far))]
    return np.exp2(a.ravel()).repeat(32)


BF16 = ml_dtypes.bfloat16


def bf(x):
    return np.asarray(x, np.float32).astype(BF16)


def f64(x):
    return np.asarray(x).astype(np.float64)


B, S, HIDDEN, Q_LORA, NUM_HEADS, QK_NOPE, QK_ROPE, KV_LORA = 2, 64, 512, 512, 16, 128, 64, 64
QK_HEAD = QK_NOPE + QK_ROPE


def rotate_half(t):
    d = t.shape[-1] // 2
    return np.concatenate([-t[..., d:], t[..., :d]], axis=-1)


def setup_inputs():
    s, t = mx_kscale(HIDDEN), mx_kscale(Q_LORA)
    x = bf(np.random.standard_normal((B, S, HIDDEN)) * s)
    cos = bf(np.random.uniform(size=(B, S, QK_ROPE)))
    sin = bf(np.random.uniform(size=(B, S, QK_ROPE)))
    Wqa = bf(np.random.standard_normal((Q_LORA, HIDDEN)) / np.sqrt(HIDDEN) * t[:, None] / s)
    Wqb = bf(np.random.standard_normal((NUM_HEADS * QK_HEAD, Q_LORA)) / np.sqrt(Q_LORA) / t)
    Wkva = bf(np.random.standard_normal((KV_LORA + QK_ROPE, HIDDEN)) / np.sqrt(HIDDEN) / s)
    return {"x": x, "cos": cos, "sin": sin, "Wqa": Wqa, "Wqb": Wqb, "Wkva": Wkva}


def reference(x, cos, sin, Wqa, Wqb, Wkva):
    b, s, _ = x.shape
    xq = mxq(f64(x), 2, "e4m3")
    qa = xq @ mxq(f64(Wqa), 1, "e4m3").T
    q = (mxq(qa, 2, "e4m3") @ mxq(f64(Wqb), 1, "e4m3").T).reshape(b, s, NUM_HEADS, QK_HEAD)
    q_nope = q[..., :QK_NOPE]
    q_pe = q[..., QK_NOPE:]
    kv = xq @ mxq(f64(Wkva), 1, "e4m3").T
    compressed_kv = kv[..., :KV_LORA]
    k_pe = kv[..., KV_LORA:].reshape(b, s, 1, QK_ROPE)
    c = f64(cos)[:, :, None, :]
    sn = f64(sin)[:, :, None, :]
    q_pe_rot = q_pe * c + rotate_half(q_pe) * sn
    k_pe_rot = k_pe * c + rotate_half(k_pe) * sn
    q_out = np.concatenate([q_nope, q_pe_rot], axis=-1).reshape(b, s, -1)
    k_out = k_pe_rot.reshape(b, s, QK_ROPE)
    return np.concatenate([q_out, k_out, compressed_kv], axis=-1)

@@ -1,0 +1,241 @@
+from contextlib import ExitStack
+
+import concourse.masks as masks
+import concourse.mybir as mybir
+
+F32 = mybir.dt.float32
+BF16 = mybir.dt.bfloat16
+U32 = mybir.dt.uint32
+U8 = mybir.dt.uint8
+FP8X4 = mybir.dt.float8_e4m3fn_x4
+MULT = mybir.AluOpType.mult
+ADD = mybir.AluOpType.add
+
+P = 128
+K = 512
+PACK = 4
+PLANES_PER_BANK = 4
+HEADS = 16
+UNIT = 64
+HALF = UNIT // 2
+UNITS_PER_HEAD = 3
+Q_COLS = HEADS * UNITS_PER_HEAD * UNIT
+CHUNK = 512
+CHUNK_ROWS = [CHUNK] * (Q_COLS // CHUNK - 1) + [CHUNK // 2, CHUNK // 2]
+CHUNKS = len(CHUNK_ROWS)
+CHUNK_START = [sum(CHUNK_ROWS[:c]) for c in range(CHUNKS)]
+LEAD = 2
+LAG = 1
+
+FLOPS = 2 * P * K * (K + Q_COLS + P)
+
+
+def transpose_planes(nc, planes_psum, raw, first_plane, planes, identity):
+    words = raw[:].bitcast(F32)
+    bank = planes_psum.tile([P, planes, P], F32, tag="planes")
+    for i in range(planes):
+        plane = first_plane + i
+        slot, u = divmod(plane, 2)
+        slot_words = words[:, slot * 2 * P : (slot + 1) * 2 * P]
+        nc.tensor.transpose(bank[:, i, :], slot_words[:, u::2], identity[:])
+    return bank
+
+
+def rotary_products(nc, stream, rotary, cos_sb, sin_sb, result, heads):
+    cos_all = cos_sb[:].unsqueeze(1).to_broadcast([P, heads, UNIT])
+    sin_low = sin_sb[:, 0:HALF].unsqueeze(1).to_broadcast([P, heads, HALF])
+    sin_high = sin_sb[:, HALF:UNIT].unsqueeze(1).to_broadcast([P, heads, HALF])
+    crossed = stream.tile([P, UNITS_PER_HEAD, UNIT], F32, tag="crossed")
+    nc.vector.tensor_tensor(out=result, in0=rotary, in1=cos_all, op=MULT)
+    nc.vector.tensor_tensor(
+        out=crossed[:, 0:heads, 0:HALF], in0=rotary[:, :, HALF:UNIT], in1=sin_low, op=MULT
+    )
+    nc.vector.tensor_tensor(
+        out=crossed[:, 0:heads, HALF:UNIT], in0=rotary[:, :, 0:HALF], in1=sin_high, op=MULT
+    )
+    return crossed[:, 0:heads, :]
+
+
+def tile_mlaselfattn_s_kernel(tc, x, cos, sin, Wqa, Wqb, Wkva, out):
+    nc = tc.nc
+    out_rows = out.flatten_outer_dims()
+
+    with ExitStack() as ctx:
+        keep = ctx.enter_context(tc.tile_pool(name="keep", bufs=1))
+        stream = ctx.enter_context(tc.tile_pool(name="stream", bufs=3))
+        planes_psum = ctx.enter_context(tc.psum_pool(name="planes_psum", bufs=4))
+        sums_psum = ctx.enter_context(tc.psum_pool(name="sums_psum", bufs=4))
+        ctx.enter_context(tc.manual_schedule())
+
+        identity = keep.tile([P, P], F32)
+        masks.make_identity(nc, identity[:])
+
+        x_raw = keep.tile([P, K], BF16)
+        nc.sync.dma_start(out=x_raw[:], in_=x.flatten_outer_dims())
+        wqa_slots = Wqa.rearrange("(p t) h -> p t h", t=PACK)
+        wqa_raw = []
+        for u in range(2):
+            raw = keep.tile([P, 2 * K], BF16, name="wqa_raw%d" % u)
+            nc.sync.dma_start(
+                out=raw[:].rearrange("p (e h) -> p e h", e=2),
+                in_=wqa_slots[:, 2 * u : 2 * u + 2, :],
+            )
+            wqa_raw.append(raw)
+        kva_raw = keep.tile([P, K], BF16)
+        nc.sync.dma_start(out=kva_raw[:], in_=Wkva)
+        wqb_raw = []
+        for c in range(CHUNKS):
+            raw = keep.tile([P, CHUNK_ROWS[c] // P * K], BF16, name="wqb_raw%d" % c)
+            nc.sync.dma_start(
+                out=raw[:],
+                in_=Wqb[CHUNK_START[c] : CHUNK_START[c] + CHUNK_ROWS[c], :].rearrange(
+                    "(p j) k -> p (j k)", p=P
+                ),
+            )
+            wqb_raw.append(raw)
+        cos_sb = keep.tile([P, UNIT], BF16)
+        sin_sb = keep.tile([P, UNIT], BF16)
+        nc.scalar.dma_start(out=cos_sb[:], in_=cos.flatten_outer_dims())
+        nc.scalar.dma_start(out=sin_sb[:], in_=sin.flatten_outer_dims())
+
+        x_codes = keep.tile([P, P], U32, align_bytes=64)
+        x_scales = keep.tile([P, P], U8, align_bytes=64)
+        kva_codes = keep.tile([P, P], U32, align_bytes=64)
+        kva_scales = keep.tile([P, P], U8, align_bytes=64)
+        wqa_codes = keep.tile([P, K], U32, align_bytes=64)
+        wqa_scales = keep.tile([P, K], U8, align_bytes=64)
+        qa_codes = keep.tile([P, P], U32, align_bytes=64)
+        qa_scales = keep.tile([P, P], U8, align_bytes=64)
+        wqb_codes = keep.tile([P, Q_COLS], U32, align_bytes=64)
+        wqb_scales = keep.tile([P, Q_COLS], U8, align_bytes=64)
+        out_sb = keep.tile([P, Q_COLS + 2 * UNIT], F32)
+
+        def prepare_blocks(raw, slots, codes, scales):
+            bank = transpose_planes(nc, planes_psum, raw, 0, 2 * slots, identity)
+            grouped = stream.tile([P, slots * P * PACK], BF16, tag="grouped_blocks", align_bytes=64)
+            nc.scalar.copy(
+                out=grouped[:].bitcast(F32).rearrange("k (r c u) -> k r c u", r=slots, u=2),
+                in_=bank[:].rearrange("k (r u) c -> k r c u", u=2),
+            )
+            nc.vector.quantize_mx(out=codes.bitcast(FP8X4), scales=scales, in_=grouped[:])
+
+        grouped_chunks = {}
+
+        def transpose_chunk(c):
+            planes = 2 * CHUNK_ROWS[c] // P
+            grouped = stream.tile(
+                [P, CHUNK_ROWS[c] * PACK], BF16, tag="grouped_chunk", name="grouped%d" % c,
+                align_bytes=64,
+            )
+            grouped_words = grouped[:].bitcast(F32).rearrange("k (c m) -> k c m", m=planes)
+            for first in range(0, planes, PLANES_PER_BANK):
+                count = min(PLANES_PER_BANK, planes - first)
+                bank = transpose_planes(nc, planes_psum, wqb_raw[c], first, count, identity)
+                nc.scalar.copy(
+                    out=grouped_words[:, :, first : first + count],
+                    in_=bank[:].rearrange("k m c -> k c m"),
+                )
+            grouped_chunks[c] = grouped
+
+        def chunk_cols(c):
+            return slice(CHUNK_START[c], CHUNK_START[c] + CHUNK_ROWS[c])
+
+        def quantise_chunk(c):
+            nc.vector.quantize_mx(
+                out=wqb_codes[:, chunk_cols(c)].bitcast(FP8X4),
+                scales=wqb_scales[:, chunk_cols(c)],
+                in_=grouped_chunks[c][:],
+            )
+
+        def multiply_chunk(c):
+            q_ps = sums_psum.tile([P, CHUNK_ROWS[c]], F32, tag="sums")
+            nc.tensor.matmul_mx(
+                out=q_ps[:],
+                lhsT=qa_codes[:].bitcast(FP8X4),
+                lhsT_scale=qa_scales[:],
+                rhs=wqb_codes[:, chunk_cols(c)].bitcast(FP8X4),
+                rhs_scale=wqb_scales[:, chunk_cols(c)],
+                start=True,
+                stop=True,
+            )
+            return q_ps
+
+        def chunk_parts(c, q_ps):
+            q_units = q_ps[:].rearrange("p (g w) -> p g w", w=UNIT)
+            out_units = out_sb[:, chunk_cols(c)].rearrange("p (g w) -> p g w", w=UNIT)
+            first = [(part - CHUNK_START[c] // UNIT) % UNITS_PER_HEAD for part in range(UNITS_PER_HEAD)]
+            return [
+                (q_units[:, f::UNITS_PER_HEAD, :], out_units[:, f::UNITS_PER_HEAD, :]) for f in first
+            ]
+
+        def multiply_rotary(rotary, rotated):
+            crossed = rotary_products(nc, stream, rotary, cos_sb, sin_sb, rotated, rotary.shape[1])
+            return rotated, crossed
+
+        def add_rotary(products):
+            rotated, crossed = products
+            nc.vector.tensor_tensor(out=rotated, in0=rotated, in1=crossed, op=ADD)
+
+        prepare_blocks(x_raw, 1, x_codes[:], x_scales[:])
+        for u in range(2):
+            cols = slice(u * 2 * P, (u + 1) * 2 * P)
+            prepare_blocks(wqa_raw[u], 2, wqa_codes[:, cols], wqa_scales[:, cols])
+        prepare_blocks(kva_raw, 1, kva_codes[:], kva_scales[:])
+        transpose_chunk(0)
+
+        qaT_ps = sums_psum.tile([P, PACK, P], F32, tag="sums")
+        for t in range(PACK):
+            nc.tensor.matmul_mx(
+                out=qaT_ps[:, t, :],
+                lhsT=wqa_codes[:, t * P : (t + 1) * P].bitcast(FP8X4),
+                lhsT_scale=wqa_scales[:, t * P : (t + 1) * P],
+                rhs=x_codes[:].bitcast(FP8X4),
+                rhs_scale=x_scales[:],
+                start=True,
+                stop=True,
+            )
+        kv_ps = sums_psum.tile([P, 2, UNIT], F32, tag="sums")
+        nc.tensor.matmul_mx(
+            out=kv_ps[:].rearrange("p g w -> p (g w)"),
+            lhsT=x_codes[:].bitcast(FP8X4),
+            lhsT_scale=x_scales[:],
+            rhs=kva_codes[:].bitcast(FP8X4),
+            rhs_scale=kva_scales[:],
+            start=True,
+            stop=True,
+        )
+        qa_grouped = keep.tile([P, P, PACK], BF16, align_bytes=64)
+        nc.vector.tensor_copy(out=qa_grouped[:], in_=qaT_ps[:].rearrange("k t n -> k n t"))
+        quantise_chunk(0)
+        nc.vector.quantize_mx(
+            out=qa_codes[:].bitcast(FP8X4),
+            scales=qa_scales[:],
+            in_=qa_grouped[:].rearrange("k n t -> k (n t)"),
+        )
+        transpose_chunk(1)
+        tail_units = out_sb[:, Q_COLS : Q_COLS + 2 * UNIT].rearrange("p (g w) -> p g w", w=UNIT)
+        nc.scalar.copy(out=tail_units[:, 1:2, :], in_=kv_ps[:, 0:1, :])
+        nc.vector.tensor_scalar_mul(out=sin_sb[:, 0:HALF], in0=sin_sb[:, 0:HALF], scalar1=-1.0)
+        products = {-LAG: multiply_rotary(kv_ps[:, 1:2, :], tail_units[:, 0:1, :])}
+
+        parts = {}
+        for step in range(CHUNKS + LAG):
+            ahead = step + LEAD
+            done = step - LAG
+            if ahead < CHUNKS:
+                transpose_chunk(ahead)
+            if step < CHUNKS:
+                parts[step] = chunk_parts(step, multiply_chunk(step))
+            if step + 1 < CHUNKS:
+                quantise_chunk(step + 1)
+            add_rotary(products[done])
+            if step < CHUNKS:
+                products[step] = multiply_rotary(parts[step][2][0], parts[step][2][1])
+            if done >= 0:
+                for part in range(UNITS_PER_HEAD - 1):
+                    nc.scalar.copy(out=parts[done][part][1], in_=parts[done][part][0])
+                first_col = CHUNK_START[done]
+                last_col = CHUNK_START[done + 1] if done + 1 < CHUNKS else Q_COLS + 2 * UNIT
+                nc.sync.dma_start(
+                    out=out_rows[:, first_col:last_col], in_=out_sb[:, first_col:last_col]
+                )

@@ -41,19 +41,18 @@ def transpose_planes(nc, planes_psum, raw, first_plane, planes, identity):
     return bank
 
 
-def rotary_products(nc, stream, rotary, cos_sb, sin_sb, result, heads):
-    cos_all = cos_sb[:].unsqueeze(1).to_broadcast([P, heads, UNIT])
-    sin_low = sin_sb[:, 0:HALF].unsqueeze(1).to_broadcast([P, heads, HALF])
-    sin_high = sin_sb[:, HALF:UNIT].unsqueeze(1).to_broadcast([P, heads, HALF])
-    crossed = stream.tile([P, UNITS_PER_HEAD, UNIT], F32, tag="crossed")
-    nc.vector.tensor_tensor(out=result, in0=rotary, in1=cos_all, op=MULT)
-    nc.vector.tensor_tensor(
-        out=crossed[:, 0:heads, 0:HALF], in0=rotary[:, :, HALF:UNIT], in1=sin_low, op=MULT
-    )
-    nc.vector.tensor_tensor(
-        out=crossed[:, 0:heads, HALF:UNIT], in0=rotary[:, :, 0:HALF], in1=sin_high, op=MULT
-    )
-    return crossed[:, 0:heads, :]
+def rotary_products(nc, stream, rotary, cos_sb, sin_sb, heads):
+    shape = [P, heads, 2, HALF]
+    terms = stream.tile([P, 2, UNITS_PER_HEAD, UNIT], F32, tag="terms")
+    halves = rotary.rearrange("p g (h i) -> p g h i", h=2)
+    for term, in0, table in ((0, halves, cos_sb), (1, halves[:, :, ::-1, :], sin_sb)):
+        nc.vector.tensor_tensor(
+            out=terms[:, term, 0:heads, :].rearrange("p g (h i) -> p g h i", h=2),
+            in0=in0,
+            in1=table[:].unsqueeze(1).to_broadcast(shape),
+            op=MULT,
+        )
+    return terms[:, :, 0:heads, :]
 
 
 def tile_mlaselfattn_s_kernel(tc, x, cos, sin, Wqa, Wqb, Wkva, out):
@@ -93,10 +92,10 @@ def tile_mlaselfattn_s_kernel(tc, x, cos, sin, Wqa, Wqb, Wkva, out):
                 ),
             )
             wqb_raw.append(raw)
-        cos_sb = keep.tile([P, UNIT], BF16)
-        sin_sb = keep.tile([P, UNIT], BF16)
-        nc.scalar.dma_start(out=cos_sb[:], in_=cos.flatten_outer_dims())
-        nc.scalar.dma_start(out=sin_sb[:], in_=sin.flatten_outer_dims())
+        cos_sb = keep.tile([P, 2, HALF], BF16)
+        sin_sb = keep.tile([P, 2, HALF], BF16)
+        nc.scalar.dma_start(out=cos_sb[:].rearrange("p o i -> p (o i)"), in_=cos.flatten_outer_dims())
+        nc.scalar.dma_start(out=sin_sb[:].rearrange("p o i -> p (o i)"), in_=sin.flatten_outer_dims())
 
         x_codes = keep.tile([P, P], U32, align_bytes=64)
         x_scales = keep.tile([P, P], U8, align_bytes=64)
@@ -169,12 +168,11 @@ def tile_mlaselfattn_s_kernel(tc, x, cos, sin, Wqa, Wqb, Wkva, out):
             ]
 
         def multiply_rotary(rotary, rotated):
-            crossed = rotary_products(nc, stream, rotary, cos_sb, sin_sb, rotated, rotary.shape[1])
-            return rotated, crossed
+            return rotated, rotary_products(nc, stream, rotary, cos_sb, sin_sb, rotary.shape[1])
 
         def add_rotary(products):
-            rotated, crossed = products
-            nc.vector.tensor_tensor(out=rotated, in0=rotated, in1=crossed, op=ADD)
+            rotated, terms = products
+            nc.vector.tensor_tensor(out=rotated, in0=terms[:, 0], in1=terms[:, 1], op=ADD)
 
         prepare_blocks(x_raw, 1, x_codes[:], x_scales[:])
         for u in range(2):
@@ -205,7 +203,7 @@ def tile_mlaselfattn_s_kernel(tc, x, cos, sin, Wqa, Wqb, Wkva, out):
             stop=True,
         )
         qa_grouped = keep.tile([P, P, PACK], BF16, align_bytes=64)
-        nc.vector.tensor_copy(out=qa_grouped[:], in_=qaT_ps[:].rearrange("k t n -> k n t"))
+        nc.scalar.copy(out=qa_grouped[:], in_=qaT_ps[:].rearrange("k t n -> k n t"))
         quantise_chunk(0)
         nc.vector.quantize_mx(
             out=qa_codes[:].bitcast(FP8X4),
@@ -215,7 +213,7 @@ def tile_mlaselfattn_s_kernel(tc, x, cos, sin, Wqa, Wqb, Wkva, out):
         transpose_chunk(1)
         tail_units = out_sb[:, Q_COLS : Q_COLS + 2 * UNIT].rearrange("p (g w) -> p g w", w=UNIT)
         nc.scalar.copy(out=tail_units[:, 1:2, :], in_=kv_ps[:, 0:1, :])
-        nc.vector.tensor_scalar_mul(out=sin_sb[:, 0:HALF], in0=sin_sb[:, 0:HALF], scalar1=-1.0)
+        nc.vector.tensor_scalar_mul(out=sin_sb[:, 0, :], in0=sin_sb[:, 0, :], scalar1=-1.0)
         products = {-LAG: multiply_rotary(kv_ps[:, 1:2, :], tail_units[:, 0:1, :])}
 
         parts = {}

@@ -69,8 +69,9 @@ def tile_mlaselfattn_s_kernel(tc, x, cos, sin, Wqa, Wqb, Wkva, out):
         identity = keep.tile([P, P], F32)
         masks.make_identity(nc, identity[:])
 
-        x_raw = keep.tile([P, K], BF16)
-        nc.sync.dma_start(out=x_raw[:], in_=x.flatten_outer_dims())
+        xkva_raw = keep.tile([P, 2 * K], BF16)
+        nc.sync.dma_start(out=xkva_raw[:, 0:K], in_=x.flatten_outer_dims())
+        nc.sync.dma_start(out=xkva_raw[:, K:], in_=Wkva)
         wqa_slots = Wqa.rearrange("(p t) h -> p t h", t=PACK)
         wqa_raw = []
         for u in range(2):
@@ -80,10 +81,15 @@ def tile_mlaselfattn_s_kernel(tc, x, cos, sin, Wqa, Wqb, Wkva, out):
                 in_=wqa_slots[:, 2 * u : 2 * u + 2, :],
             )
             wqa_raw.append(raw)
-        kva_raw = keep.tile([P, K], BF16)
-        nc.sync.dma_start(out=kva_raw[:], in_=Wkva)
+        cos_sb = keep.tile([P, 2, HALF], BF16)
+        sin_sb = keep.tile([P, 2, HALF], BF16)
         wqb_raw = []
         for c in range(CHUNKS):
+            if c == 1:
+                for table, source in ((cos_sb, cos), (sin_sb, sin)):
+                    nc.sync.dma_start(
+                        out=table[:].rearrange("p o i -> p (o i)"), in_=source.flatten_outer_dims()
+                    )
             raw = keep.tile([P, CHUNK_ROWS[c] // P * K], BF16, name="wqb_raw%d" % c)
             nc.sync.dma_start(
                 out=raw[:],
@@ -92,15 +98,11 @@ def tile_mlaselfattn_s_kernel(tc, x, cos, sin, Wqa, Wqb, Wkva, out):
                 ),
             )
             wqb_raw.append(raw)
-        cos_sb = keep.tile([P, 2, HALF], BF16)
-        sin_sb = keep.tile([P, 2, HALF], BF16)
-        nc.scalar.dma_start(out=cos_sb[:].rearrange("p o i -> p (o i)"), in_=cos.flatten_outer_dims())
-        nc.scalar.dma_start(out=sin_sb[:].rearrange("p o i -> p (o i)"), in_=sin.flatten_outer_dims())
 
-        x_codes = keep.tile([P, P], U32, align_bytes=64)
-        x_scales = keep.tile([P, P], U8, align_bytes=64)
-        kva_codes = keep.tile([P, P], U32, align_bytes=64)
-        kva_scales = keep.tile([P, P], U8, align_bytes=64)
+        xkva_codes = keep.tile([P, 2 * P], U32, align_bytes=64)
+        xkva_scales = keep.tile([P, 2 * P], U8, align_bytes=64)
+        x_codes, kva_codes = xkva_codes[:, 0:P], xkva_codes[:, P:]
+        x_scales, kva_scales = xkva_scales[:, 0:P], xkva_scales[:, P:]
         wqa_codes = keep.tile([P, K], U32, align_bytes=64)
         wqa_scales = keep.tile([P, K], U8, align_bytes=64)
         qa_codes = keep.tile([P, P], U32, align_bytes=64)
@@ -174,11 +176,10 @@ def tile_mlaselfattn_s_kernel(tc, x, cos, sin, Wqa, Wqb, Wkva, out):
             rotated, terms = products
             nc.vector.tensor_tensor(out=rotated, in0=terms[:, 0], in1=terms[:, 1], op=ADD)
 
-        prepare_blocks(x_raw, 1, x_codes[:], x_scales[:])
+        prepare_blocks(xkva_raw, 2, xkva_codes[:], xkva_scales[:])
         for u in range(2):
             cols = slice(u * 2 * P, (u + 1) * 2 * P)
             prepare_blocks(wqa_raw[u], 2, wqa_codes[:, cols], wqa_scales[:, cols])
-        prepare_blocks(kva_raw, 1, kva_codes[:], kva_scales[:])
         transpose_chunk(0)
 
         qaT_ps = sums_psum.tile([P, PACK, P], F32, tag="sums")
@@ -187,18 +188,18 @@ def tile_mlaselfattn_s_kernel(tc, x, cos, sin, Wqa, Wqb, Wkva, out):
                 out=qaT_ps[:, t, :],
                 lhsT=wqa_codes[:, t * P : (t + 1) * P].bitcast(FP8X4),
                 lhsT_scale=wqa_scales[:, t * P : (t + 1) * P],
-                rhs=x_codes[:].bitcast(FP8X4),
-                rhs_scale=x_scales[:],
+                rhs=x_codes.bitcast(FP8X4),
+                rhs_scale=x_scales,
                 start=True,
                 stop=True,
             )
         kv_ps = sums_psum.tile([P, 2, UNIT], F32, tag="sums")
         nc.tensor.matmul_mx(
             out=kv_ps[:].rearrange("p g w -> p (g w)"),
-            lhsT=x_codes[:].bitcast(FP8X4),
-            lhsT_scale=x_scales[:],
-            rhs=kva_codes[:].bitcast(FP8X4),
-            rhs_scale=kva_scales[:],
+            lhsT=x_codes.bitcast(FP8X4),
+            lhsT_scale=x_scales,
+            rhs=kva_codes.bitcast(FP8X4),
+            rhs_scale=kva_scales,
             start=True,
             stop=True,
         )
@@ -213,7 +214,7 @@ def tile_mlaselfattn_s_kernel(tc, x, cos, sin, Wqa, Wqb, Wkva, out):
         transpose_chunk(1)
         tail_units = out_sb[:, Q_COLS : Q_COLS + 2 * UNIT].rearrange("p (g w) -> p g w", w=UNIT)
         nc.scalar.copy(out=tail_units[:, 1:2, :], in_=kv_ps[:, 0:1, :])
-        nc.vector.tensor_scalar_mul(out=sin_sb[:, 0, :], in0=sin_sb[:, 0, :], scalar1=-1.0)
+        nc.scalar.mul(out=sin_sb[:, 0, :], in_=sin_sb[:, 0, :], mul=-1.0)
         products = {-LAG: multiply_rotary(kv_ps[:, 1:2, :], tail_units[:, 0:1, :])}
 
         parts = {}
@@ -227,13 +228,15 @@ def tile_mlaselfattn_s_kernel(tc, x, cos, sin, Wqa, Wqb, Wkva, out):
             if step + 1 < CHUNKS:
                 quantise_chunk(step + 1)
             add_rotary(products[done])
+            if done < 0:
+                nc.sync.dma_start(out=out_rows[:, Q_COLS:], in_=out_sb[:, Q_COLS:])
             if step < CHUNKS:
                 products[step] = multiply_rotary(parts[step][2][0], parts[step][2][1])
             if done >= 0:
                 for part in range(UNITS_PER_HEAD - 1):
                     nc.scalar.copy(out=parts[done][part][1], in_=parts[done][part][0])
                 first_col = CHUNK_START[done]
-                last_col = CHUNK_START[done + 1] if done + 1 < CHUNKS else Q_COLS + 2 * UNIT
+                last_col = first_col + CHUNK_ROWS[done]
                 nc.sync.dma_start(
                     out=out_rows[:, first_col:last_col], in_=out_sb[:, first_col:last_col]
                 )

@@ -24,7 +24,7 @@ CHUNK = 512
 CHUNK_ROWS = [CHUNK] * (Q_COLS // CHUNK - 1) + [CHUNK // 2, CHUNK // 2]
 CHUNKS = len(CHUNK_ROWS)
 CHUNK_START = [sum(CHUNK_ROWS[:c]) for c in range(CHUNKS)]
-LEAD = 2
+LEAD_ROWS = 2 * CHUNK
 LAG = 1
 
 FLOPS = 2 * P * K * (K + Q_COLS + P)
@@ -218,12 +218,14 @@ def tile_mlaselfattn_s_kernel(tc, x, cos, sin, Wqa, Wqb, Wkva, out):
         products = {-LAG: multiply_rotary(kv_ps[:, 1:2, :], tail_units[:, 0:1, :])}
 
         parts = {}
+        transposed = 2
         for step in range(CHUNKS + LAG):
-            ahead = step + LEAD
             done = step - LAG
-            if ahead < CHUNKS:
-                transpose_chunk(ahead)
             if step < CHUNKS:
+                limit = min(CHUNK_START[step] + CHUNK_ROWS[step] + LEAD_ROWS, Q_COLS)
+                while transposed < CHUNKS and CHUNK_START[transposed] + CHUNK_ROWS[transposed] <= limit:
+                    transpose_chunk(transposed)
+                    transposed += 1
                 parts[step] = chunk_parts(step, multiply_chunk(step))
             if step + 1 < CHUNKS:
                 quantise_chunk(step + 1)

@@ -23,7 +23,7 @@ Q_COLS = HEADS * UNITS_PER_HEAD * UNIT
 CHUNK = 512
 CHUNK_ROWS = [CHUNK] * (Q_COLS // CHUNK - 1) + [CHUNK // 2, CHUNK // 2]
 CHUNKS = len(CHUNK_ROWS)
-CHUNK_START = [sum(CHUNK_ROWS[:c]) for c in range(CHUNKS)]
+CHUNK_START = [c * CHUNK for c in range(CHUNKS - 2)] + [Q_COLS - CHUNK // 2, Q_COLS - CHUNK]
 LEAD_ROWS = 2 * CHUNK
 LAG = 1
 
@@ -148,23 +148,43 @@ def tile_mlaselfattn_s_kernel(tc, x, cos, sin, Wqa, Wqb, Wkva, out):
                 in_=grouped_chunks[c][:],
             )
 
-        def multiply_chunk(c):
-            q_ps = sums_psum.tile([P, CHUNK_ROWS[c]], F32, tag="sums")
+        def multiply_into(out, cols):
             nc.tensor.matmul_mx(
-                out=q_ps[:],
+                out=out,
                 lhsT=qa_codes[:].bitcast(FP8X4),
                 lhsT_scale=qa_scales[:],
-                rhs=wqb_codes[:, chunk_cols(c)].bitcast(FP8X4),
-                rhs_scale=wqb_scales[:, chunk_cols(c)],
+                rhs=wqb_codes[:, cols].bitcast(FP8X4),
+                rhs_scale=wqb_scales[:, cols],
                 start=True,
                 stop=True,
             )
-            return q_ps
+
+        def multiply_chunk(c):
+            q_ps = sums_psum.tile([P, CHUNK_ROWS[c]], F32, tag="sums")
+            multiply_into(q_ps[:], chunk_cols(c))
+            return chunk_parts(c, q_ps)
+
+        def multiply_last_chunk(c):
+            rotary = sums_psum.tile([P, 1, UNIT], F32, tag="sums")
+            passing = sums_psum.tile([P, 3, UNIT], F32, tag="sums")
+            start = CHUNK_START[c]
+            multiply_into(rotary[:, 0, :], slice(start + UNIT, start + 2 * UNIT))
+            multiply_into(passing[:, 0, :], slice(start, start + UNIT))
+            pair = passing[:, 1:3, :]
+            multiply_into(
+                pair.rearrange("p g w -> p (g w)"), slice(start + 2 * UNIT, start + 4 * UNIT)
+            )
+            out_units = out_sb[:, chunk_cols(c)].rearrange("p (g w) -> p g w", w=UNIT)
+            return [
+                (rotary[:], out_units[:, 1:2, :]),
+                (passing[:, 0:1, :], out_units[:, 0:1, :]),
+                (pair, out_units[:, 2:4, :]),
+            ]
 
         def chunk_parts(c, q_ps):
             q_units = q_ps[:].rearrange("p (g w) -> p g w", w=UNIT)
             out_units = out_sb[:, chunk_cols(c)].rearrange("p (g w) -> p g w", w=UNIT)
-            first = [(part - CHUNK_START[c] // UNIT) % UNITS_PER_HEAD for part in range(UNITS_PER_HEAD)]
+            first = [(part - CHUNK_START[c] // UNIT) % UNITS_PER_HEAD for part in (2, 0, 1)]
             return [
                 (q_units[:, f::UNITS_PER_HEAD, :], out_units[:, f::UNITS_PER_HEAD, :]) for f in first
             ]
@@ -222,21 +242,22 @@ def tile_mlaselfattn_s_kernel(tc, x, cos, sin, Wqa, Wqb, Wkva, out):
         for step in range(CHUNKS + LAG):
             done = step - LAG
             if step < CHUNKS:
-                limit = min(CHUNK_START[step] + CHUNK_ROWS[step] + LEAD_ROWS, Q_COLS)
-                while transposed < CHUNKS and CHUNK_START[transposed] + CHUNK_ROWS[transposed] <= limit:
+                limit = sum(CHUNK_ROWS[: step + 1]) + LEAD_ROWS
+                while transposed < CHUNKS and sum(CHUNK_ROWS[: transposed + 1]) <= limit:
                     transpose_chunk(transposed)
                     transposed += 1
-                parts[step] = chunk_parts(step, multiply_chunk(step))
+                multiply = multiply_chunk if step + 1 < CHUNKS else multiply_last_chunk
+                parts[step] = multiply(step)
             if step + 1 < CHUNKS:
                 quantise_chunk(step + 1)
             add_rotary(products[done])
             if done < 0:
                 nc.sync.dma_start(out=out_rows[:, Q_COLS:], in_=out_sb[:, Q_COLS:])
             if step < CHUNKS:
-                products[step] = multiply_rotary(parts[step][2][0], parts[step][2][1])
+                products[step] = multiply_rotary(parts[step][0][0], parts[step][0][1])
             if done >= 0:
-                for part in range(UNITS_PER_HEAD - 1):
-                    nc.scalar.copy(out=parts[done][part][1], in_=parts[done][part][0])
+                for sums, result in parts[done][1:]:
+                    nc.scalar.copy(out=result, in_=sums)
                 first_col = CHUNK_START[done]
                 last_col = first_col + CHUNK_ROWS[done]
                 nc.sync.dma_start(

from contextlib import ExitStack

import concourse.masks as masks
import concourse.mybir as mybir

F32 = mybir.dt.float32
BF16 = mybir.dt.bfloat16
U32 = mybir.dt.uint32
U8 = mybir.dt.uint8
FP8X4 = mybir.dt.float8_e4m3fn_x4
MULT = mybir.AluOpType.mult
ADD = mybir.AluOpType.add

P = 128
K = 512
PACK = 4
PLANES_PER_BANK = 4
HEADS = 16
UNIT = 64
HALF = UNIT // 2
UNITS_PER_HEAD = 3
Q_COLS = HEADS * UNITS_PER_HEAD * UNIT
CHUNK = 512
CHUNK_ROWS = [CHUNK] * (Q_COLS // CHUNK - 1) + [CHUNK // 2, CHUNK // 2]
CHUNKS = len(CHUNK_ROWS)
CHUNK_START = [c * CHUNK for c in range(CHUNKS - 2)] + [Q_COLS - CHUNK // 2, Q_COLS - CHUNK]
LEAD_ROWS = 2 * CHUNK
LAG = 1

FLOPS = 2 * P * K * (K + Q_COLS + P)


def transpose_planes(nc, planes_psum, raw, first_plane, planes, identity):
    words = raw[:].bitcast(F32)
    bank = planes_psum.tile([P, planes, P], F32, tag="planes")
    for i in range(planes):
        plane = first_plane + i
        slot, u = divmod(plane, 2)
        slot_words = words[:, slot * 2 * P : (slot + 1) * 2 * P]
        nc.tensor.transpose(bank[:, i, :], slot_words[:, u::2], identity[:])
    return bank


def rotary_products(nc, stream, rotary, cos_sb, sin_sb, heads):
    shape = [P, heads, 2, HALF]
    terms = stream.tile([P, 2, UNITS_PER_HEAD, UNIT], F32, tag="terms")
    halves = rotary.rearrange("p g (h i) -> p g h i", h=2)
    for term, in0, table in ((0, halves, cos_sb), (1, halves[:, :, ::-1, :], sin_sb)):
        nc.vector.tensor_tensor(
            out=terms[:, term, 0:heads, :].rearrange("p g (h i) -> p g h i", h=2),
            in0=in0,
            in1=table[:].unsqueeze(1).to_broadcast(shape),
            op=MULT,
        )
    return terms[:, :, 0:heads, :]


def tile_mlaselfattn_s_kernel(tc, x, cos, sin, Wqa, Wqb, Wkva, out):
    nc = tc.nc
    out_rows = out.flatten_outer_dims()

    with ExitStack() as ctx:
        keep = ctx.enter_context(tc.tile_pool(name="keep", bufs=1))
        stream = ctx.enter_context(tc.tile_pool(name="stream", bufs=3))
        planes_psum = ctx.enter_context(tc.psum_pool(name="planes_psum", bufs=4))
        sums_psum = ctx.enter_context(tc.psum_pool(name="sums_psum", bufs=4))
        ctx.enter_context(tc.manual_schedule())

        identity = keep.tile([P, P], F32)
        masks.make_identity(nc, identity[:])

        xkva_raw = keep.tile([P, 2 * K], BF16)
        nc.sync.dma_start(out=xkva_raw[:, 0:K], in_=x.flatten_outer_dims())
        nc.sync.dma_start(out=xkva_raw[:, K:], in_=Wkva)
        wqa_slots = Wqa.rearrange("(p t) h -> p t h", t=PACK)
        wqa_raw = []
        for u in range(2):
            raw = keep.tile([P, 2 * K], BF16, name="wqa_raw%d" % u)
            nc.sync.dma_start(
                out=raw[:].rearrange("p (e h) -> p e h", e=2),
                in_=wqa_slots[:, 2 * u : 2 * u + 2, :],
            )
            wqa_raw.append(raw)
        cos_sb = keep.tile([P, 2, HALF], BF16)
        sin_sb = keep.tile([P, 2, HALF], BF16)
        wqb_raw = []
        for c in range(CHUNKS):
            if c == 1:
                for table, source in ((cos_sb, cos), (sin_sb, sin)):
                    nc.sync.dma_start(
                        out=table[:].rearrange("p o i -> p (o i)"), in_=source.flatten_outer_dims()
                    )
            raw = keep.tile([P, CHUNK_ROWS[c] // P * K], BF16, name="wqb_raw%d" % c)
            nc.sync.dma_start(
                out=raw[:],
                in_=Wqb[CHUNK_START[c] : CHUNK_START[c] + CHUNK_ROWS[c], :].rearrange(
                    "(p j) k -> p (j k)", p=P
                ),
            )
            wqb_raw.append(raw)

        xkva_codes = keep.tile([P, 2 * P], U32, align_bytes=64)
        xkva_scales = keep.tile([P, 2 * P], U8, align_bytes=64)
        x_codes, kva_codes = xkva_codes[:, 0:P], xkva_codes[:, P:]
        x_scales, kva_scales = xkva_scales[:, 0:P], xkva_scales[:, P:]
        wqa_codes = keep.tile([P, K], U32, align_bytes=64)
        wqa_scales = keep.tile([P, K], U8, align_bytes=64)
        qa_codes = keep.tile([P, P], U32, align_bytes=64)
        qa_scales = keep.tile([P, P], U8, align_bytes=64)
        wqb_codes = keep.tile([P, Q_COLS], U32, align_bytes=64)
        wqb_scales = keep.tile([P, Q_COLS], U8, align_bytes=64)
        out_sb = keep.tile([P, Q_COLS + 2 * UNIT], F32)

        def prepare_blocks(raw, slots, codes, scales):
            bank = transpose_planes(nc, planes_psum, raw, 0, 2 * slots, identity)
            grouped = stream.tile([P, slots * P * PACK], BF16, tag="grouped_blocks", align_bytes=64)
            nc.scalar.copy(
                out=grouped[:].bitcast(F32).rearrange("k (r c u) -> k r c u", r=slots, u=2),
                in_=bank[:].rearrange("k (r u) c -> k r c u", u=2),
            )
            nc.vector.quantize_mx(out=codes.bitcast(FP8X4), scales=scales, in_=grouped[:])

        grouped_chunks = {}

        def transpose_chunk(c):
            planes = 2 * CHUNK_ROWS[c] // P
            grouped = stream.tile(
                [P, CHUNK_ROWS[c] * PACK], BF16, tag="grouped_chunk", name="grouped%d" % c,
                align_bytes=64,
            )
            grouped_words = grouped[:].bitcast(F32).rearrange("k (c m) -> k c m", m=planes)
            for first in range(0, planes, PLANES_PER_BANK):
                count = min(PLANES_PER_BANK, planes - first)
                bank = transpose_planes(nc, planes_psum, wqb_raw[c], first, count, identity)
                nc.scalar.copy(
                    out=grouped_words[:, :, first : first + count],
                    in_=bank[:].rearrange("k m c -> k c m"),
                )
            grouped_chunks[c] = grouped

        def chunk_cols(c):
            return slice(CHUNK_START[c], CHUNK_START[c] + CHUNK_ROWS[c])

        def quantise_chunk(c):
            nc.vector.quantize_mx(
                out=wqb_codes[:, chunk_cols(c)].bitcast(FP8X4),
                scales=wqb_scales[:, chunk_cols(c)],
                in_=grouped_chunks[c][:],
            )

        def multiply_into(out, cols):
            nc.tensor.matmul_mx(
                out=out,
                lhsT=qa_codes[:].bitcast(FP8X4),
                lhsT_scale=qa_scales[:],
                rhs=wqb_codes[:, cols].bitcast(FP8X4),
                rhs_scale=wqb_scales[:, cols],
                start=True,
                stop=True,
            )

        def multiply_chunk(c):
            q_ps = sums_psum.tile([P, CHUNK_ROWS[c]], F32, tag="sums")
            multiply_into(q_ps[:], chunk_cols(c))
            return chunk_parts(c, q_ps)

        def multiply_last_chunk(c):
            rotary = sums_psum.tile([P, 1, UNIT], F32, tag="sums")
            passing = sums_psum.tile([P, 3, UNIT], F32, tag="sums")
            start = CHUNK_START[c]
            multiply_into(rotary[:, 0, :], slice(start + UNIT, start + 2 * UNIT))
            multiply_into(passing[:, 0, :], slice(start, start + UNIT))
            pair = passing[:, 1:3, :]
            multiply_into(
                pair.rearrange("p g w -> p (g w)"), slice(start + 2 * UNIT, start + 4 * UNIT)
            )
            out_units = out_sb[:, chunk_cols(c)].rearrange("p (g w) -> p g w", w=UNIT)
            return [
                (rotary[:], out_units[:, 1:2, :]),
                (passing[:, 0:1, :], out_units[:, 0:1, :]),
                (pair, out_units[:, 2:4, :]),
            ]

        def chunk_parts(c, q_ps):
            q_units = q_ps[:].rearrange("p (g w) -> p g w", w=UNIT)
            out_units = out_sb[:, chunk_cols(c)].rearrange("p (g w) -> p g w", w=UNIT)
            first = [(part - CHUNK_START[c] // UNIT) % UNITS_PER_HEAD for part in (2, 0, 1)]
            return [
                (q_units[:, f::UNITS_PER_HEAD, :], out_units[:, f::UNITS_PER_HEAD, :]) for f in first
            ]

        def multiply_rotary(rotary, rotated):
            return rotated, rotary_products(nc, stream, rotary, cos_sb, sin_sb, rotary.shape[1])

        def add_rotary(products):
            rotated, terms = products
            nc.vector.tensor_tensor(out=rotated, in0=terms[:, 0], in1=terms[:, 1], op=ADD)

        prepare_blocks(xkva_raw, 2, xkva_codes[:], xkva_scales[:])
        for u in range(2):
            cols = slice(u * 2 * P, (u + 1) * 2 * P)
            prepare_blocks(wqa_raw[u], 2, wqa_codes[:, cols], wqa_scales[:, cols])
        transpose_chunk(0)

        qaT_ps = sums_psum.tile([P, PACK, P], F32, tag="sums")
        for t in range(PACK):
            nc.tensor.matmul_mx(
                out=qaT_ps[:, t, :],
                lhsT=wqa_codes[:, t * P : (t + 1) * P].bitcast(FP8X4),
                lhsT_scale=wqa_scales[:, t * P : (t + 1) * P],
                rhs=x_codes.bitcast(FP8X4),
                rhs_scale=x_scales,
                start=True,
                stop=True,
            )
        kv_ps = sums_psum.tile([P, 2, UNIT], F32, tag="sums")
        nc.tensor.matmul_mx(
            out=kv_ps[:].rearrange("p g w -> p (g w)"),
            lhsT=x_codes.bitcast(FP8X4),
            lhsT_scale=x_scales,
            rhs=kva_codes.bitcast(FP8X4),
            rhs_scale=kva_scales,
            start=True,
            stop=True,
        )
        qa_grouped = keep.tile([P, P, PACK], BF16, align_bytes=64)
        nc.scalar.copy(out=qa_grouped[:], in_=qaT_ps[:].rearrange("k t n -> k n t"))
        quantise_chunk(0)
        nc.vector.quantize_mx(
            out=qa_codes[:].bitcast(FP8X4),
            scales=qa_scales[:],
            in_=qa_grouped[:].rearrange("k n t -> k (n t)"),
        )
        transpose_chunk(1)
        tail_units = out_sb[:, Q_COLS : Q_COLS + 2 * UNIT].rearrange("p (g w) -> p g w", w=UNIT)
        nc.scalar.copy(out=tail_units[:, 1:2, :], in_=kv_ps[:, 0:1, :])
        nc.scalar.mul(out=sin_sb[:, 0, :], in_=sin_sb[:, 0, :], mul=-1.0)
        products = {-LAG: multiply_rotary(kv_ps[:, 1:2, :], tail_units[:, 0:1, :])}

        parts = {}
        transposed = 2
        for step in range(CHUNKS + LAG):
            done = step - LAG
            if step < CHUNKS:
                limit = sum(CHUNK_ROWS[: step + 1]) + LEAD_ROWS
                while transposed < CHUNKS and sum(CHUNK_ROWS[: transposed + 1]) <= limit:
                    transpose_chunk(transposed)
                    transposed += 1
                multiply = multiply_chunk if step + 1 < CHUNKS else multiply_last_chunk
                parts[step] = multiply(step)
            if step + 1 < CHUNKS:
                quantise_chunk(step + 1)
            add_rotary(products[done])
            if done < 0:
                nc.sync.dma_start(out=out_rows[:, Q_COLS:], in_=out_sb[:, Q_COLS:])
            if step < CHUNKS:
                products[step] = multiply_rotary(parts[step][0][0], parts[step][0][1])
            if done >= 0:
                for sums, result in parts[done][1:]:
                    nc.scalar.copy(out=result, in_=sums)
                first_col = CHUNK_START[done]
                last_col = first_col + CHUNK_ROWS[done]
                nc.sync.dma_start(
                    out=out_rows[:, first_col:last_col], in_=out_sb[:, first_col:last_col]
                )
